import numpy as np
import ml_dtypes


def mxq(x, axis, fmt="e4m3"):
    dtype, down = {"e4m3": (ml_dtypes.float8_e4m3fn, 7), "e5m2": (ml_dtypes.float8_e5m2, 14)}[fmt]
    v = np.moveaxis(np.asarray(x, np.float32).astype(ml_dtypes.bfloat16).astype(np.float64), axis, -1)
    blocks = v.reshape(v.shape[:-1] + (-1, 32))
    amax = np.abs(blocks).max(-1, keepdims=True)
    byte = np.maximum(np.where(amax > 0, np.frexp(amax)[1] - 1 + 127, 0) - down, 1)
    scale = np.exp2(byte - 127.0)
    codes = (blocks / scale).astype(np.float32).astype(dtype).astype(np.float64)
    return np.moveaxis((codes * scale).reshape(v.shape), -1, axis)


WIDE = False


def mx_kscale(k):
    if not WIDE:
        return np.ones(k)
    levels = np.array([18, -18])
    if k % 512:
        return np.exp2(np.random.permutation(np.resize(levels, k // 32))).repeat(32)
    a = np.empty((k // 512, 16))
    for p in range(k // 512):
        a[p, :8] = np.random.permutation(np.resize(levels, 8))
        for g in range(8):
            far = levels[np.abs(levels - a[p, g]) >= 10]
            a[p, g + 8] = far[np.random.randint(len(far))]
    return np.exp2(a.ravel()).repeat(32)


BF16 = ml_dtypes.bfloat16


def bf(x):
    return np.asarray(x, np.float32).astype(BF16)


def f64(x):
    return np.asarray(x).astype(np.float64)


B, SQ, SKV, DIN, Q_HEADS, KV_HEADS, DIMS = 1, 1024, 512, 2048, 4, 2, 2048
HEAD_DIM = DIMS // Q_HEADS
REP = Q_HEADS // KV_HEADS


def attention_scores(xq, xk_rep):
    qh = f64(xq).reshape(B, SQ, Q_HEADS, HEAD_DIM).transpose(0, 2, 1, 3)
    kh = f64(xk_rep).reshape(B, SKV, Q_HEADS, HEAD_DIM).transpose(0, 2, 3, 1)
    return (qh @ kh) * (HEAD_DIM ** -0.5)


def row_lse(scores, mask):
    t = scores - (1.0 / f64(mask) - 1.0)
    m = t.max(-1)
    return m + np.log(np.exp(t - m[..., None]).sum(-1))


def setup_inputs():
    u = mx_kscale(SQ)
    v = mx_kscale(KV_HEADS * HEAD_DIM)
    s = mx_kscale(SKV)
    xq = bf(np.random.standard_normal((B, SQ, DIMS)) * 2.0)
    xk_rep = bf(np.repeat(np.random.standard_normal((B, SKV, KV_HEADS * HEAD_DIM)) * 1.5, REP, axis=-1))
    kv0 = bf(np.random.standard_normal((B, SKV, DIN)))
    mask0 = bf(np.random.uniform(0.25, 1.0, (1, 1, SQ, SKV)))
    Wv0 = bf(np.random.standard_normal((DIN, KV_HEADS * HEAD_DIM)) / np.sqrt(DIN))
    scores = attention_scores(xq, xk_rep)
    lse = row_lse(scores, mask0)
    mask = bf(1.0 / (1.0 / f64(mask0) - np.log(u)[:, None] + np.log(s)[None, :]))
    g = bf(np.random.standard_normal((B, SQ, DIMS)) * np.exp2(np.random.randint(-6, 1, (B, SQ, 1))) / u[None, :, None] * np.repeat(v, REP))
    return {
        "xq": xq,
        "xk_rep": xk_rep,
        "kv": bf(f64(kv0) * s[None, :, None]),
        "mask": mask,
        "Wv": bf(f64(Wv0) / v[None, :]),
        "scores": np.asarray(scores, np.float32),
        "lse": np.asarray(lse, np.float32),
        "grad_out": g,
    }


def reference(xq, xk_rep, kv, mask, Wv, scores, lse, grad_out):
    p = np.exp(f64(scores) - (1.0 / f64(mask) - 1.0) - f64(lse)[..., None])
    gh = f64(grad_out).reshape(B, SQ, Q_HEADS, HEAD_DIM).transpose(0, 2, 1, 3)
    dh = mxq(p, 2, "e4m3").transpose(0, 1, 3, 2) @ mxq(gh, 2, "e5m2")
    dxv = dh.transpose(0, 2, 1, 3).reshape(B * SKV, KV_HEADS * HEAD_DIM, REP).sum(-1)
    kvf = f64(kv).reshape(B * SKV, DIN)
    dkv = mxq(dxv, 1, "e5m2") @ mxq(f64(Wv), 1, "e4m3").T
    dWv = mxq(kvf, 0, "e4m3").T @ mxq(dxv, 0, "e5m2")
    return dkv.reshape(B, SKV, DIN), dWv

@@ -1,0 +1,460 @@
+from contextlib import ExitStack
+
+import concourse.mybir as mybir
+from concourse.masks import make_identity
+
+SQ, SKV, DIN, HEADS, DIMS, FEATS = 1024, 512, 2048, 4, 2048, 1024
+FLOPS = 2 * SQ * SKV * DIMS + 2 * 2 * SKV * DIN * FEATS
+BYTES = 2 * (SKV * DIN + SQ * SKV + DIN * FEATS + SQ * DIMS) + 4 * (HEADS * SQ * SKV + HEADS * SQ + SKV * DIN + DIN * FEATS)
+
+F32 = mybir.dt.float32
+BF16 = mybir.dt.bfloat16
+U32 = mybir.dt.uint32
+U8 = mybir.dt.uint8
+E4 = mybir.dt.float8_e4m3fn_x4
+E5 = mybir.dt.float8_e5m2_x4
+ACT = mybir.ActivationFunctionType
+ALU = mybir.AluOpType
+
+P = 128
+PACK = 4
+N = 512
+HALF = 64
+ZONE = 3 * HALF
+SLOTS = 8
+
+
+def tile_groupedqueryattention_pa_v_kernel(tc, xq, xk_rep, kv, mask, Wv, scores, lse, grad_out, out_0, out_1):
+    nc = tc.nc
+    with ExitStack() as ctx:
+        keep = ctx.enter_context(tc.tile_pool(name="keep", bufs=1))
+        flow = ctx.enter_context(tc.tile_pool(name="flow", bufs=2))
+        psum = ctx.enter_context(tc.psum_pool(name="psum", bufs=1))
+        ctx.enter_context(tc.manual_schedule())
+
+        def copy(engine, out, in_):
+            if engine is nc.scalar:
+                nc.scalar.copy(out=out, in_=in_)
+            else:
+                nc.vector.tensor_copy(out=out, in_=in_)
+
+        def bank(k):
+            return psum.tile([P, N], F32, name="bank%d" % k, tag="bank%d" % k)
+
+        def mx_tiles(pool, name, width, bufs):
+            codes = pool.tile([P, width], U32, name=name + "_codes", tag=name + "_codes", bufs=bufs, align_bytes=64)
+            scales = pool.tile([P, width], U8, name=name + "_scales", tag=name + "_scales", bufs=bufs, align_bytes=64)
+            return codes, scales
+
+        def quantize(mx, cols, fmt, values):
+            nc.vector.quantize_mx(out=mx[0][:, cols].bitcast(fmt), scales=mx[1][:, cols], in_=values)
+
+        def product(acc, lhs, lhs_cols, lhs_fmt, rhs, rhs_cols, rhs_fmt, start, stop):
+            nc.tensor.matmul_mx(
+                out=acc[:],
+                lhsT=lhs[0][:, lhs_cols].bitcast(lhs_fmt),
+                lhsT_scale=lhs[1][:, lhs_cols],
+                rhs=rhs[0][:, rhs_cols].bitcast(rhs_fmt),
+                rhs_scale=rhs[1][:, rhs_cols],
+                start=start,
+                stop=stop,
+            )
+
+        ident = keep.tile([P, P], F32, name="ident")
+        warm = keep.tile([P, 1], F32, name="warm")
+        lse_sb = keep.tile([P, 2 * HEADS, PACK], F32, name="lse_sb")
+        shift = keep.tile([P, 2 * HEADS * PACK], F32, name="shift")
+        mask_sb = [keep.tile([P, PACK * SKV], BF16, name="mask%d" % g) for g in range(2)]
+        size = [flow.tile([P, PACK * SKV], BF16, name="size%d" % g, tag="p", bufs=2, align_bytes=64) for g in range(2)]
+        recip = [keep.tile([P, PACK * SKV], F32, name="recip%d" % g) for g in range(2)]
+        g_mx = mx_tiles(keep, "g", (4 * SLOTS + 1) * ZONE, 1)
+        kv_mx = [mx_tiles(keep, "kv%d" % c, 1024, 1) for c in range(2)]
+        w_mx = [mx_tiles(keep, "w%d" % n, 1024, 1) for n in range(4)]
+        df_mx = [mx_tiles(keep, "df%d" % f, N, 1) for f in range(2)]
+        dk_mx = [mx_tiles(keep, "dk%d" % f, N, 1) for f in range(2)]
+        live = {}
+        done = []
+
+        def load_mask(g):
+            nc.sync.dma_start(
+                out=mask_sb[g][:].rearrange("p (j k) -> p j k", j=PACK),
+                in_=mask[0, 0, N * g : N * (g + 1), :].rearrange("(p j) k -> p j k", j=PACK),
+            )
+
+        def load_rows(key, rows):
+            raw = flow.tile([P, PACK, 1024], BF16, name="raw", tag="raw", bufs=5)
+            nc.sync.dma_start(out=raw[:], in_=rows.rearrange("(p j) c -> p j c", j=PACK))
+            live[key] = raw
+
+        def load_g(f, g):
+            load_rows(("g", f, g), grad_out[0, N * g : N * (g + 1), 1024 * f : 1024 * (f + 1)])
+
+        def load_g_half(f, g, a):
+            if a == 0:
+                live[("g", f, g)] = flow.tile([P, PACK, 1024], BF16, name="raw", tag="raw", bufs=5)
+            rows = grad_out[0, N * g : N * (g + 1), 1024 * f + N * a : 1024 * f + N * (a + 1)]
+            nc.sync.dma_start(
+                out=live[("g", f, g)][:, :, N * a : N * (a + 1)], in_=rows.rearrange("(p j) c -> p j c", j=PACK)
+            )
+
+        def load_kv(c):
+            load_rows(("kv", c), kv[0, :, 1024 * c : 1024 * (c + 1)])
+
+        def load_w(n):
+            load_rows(("w", n), Wv[N * n : N * (n + 1), :])
+
+        def load_scores(h, g):
+            s = flow.tile([P, PACK, SKV], F32, name="s", tag="s", bufs=3)
+            nc.sync.dma_start(out=s[:], in_=scores[0, h, N * g : N * (g + 1), :].rearrange("(p j) k -> p j k", j=PACK))
+            live[("s", h, g)] = s
+
+        def magnitude(g):
+            nc.scalar.activation(out=size[g][:], in_=mask_sb[g][:], func=ACT.Abs, scale=0.5)
+
+        def clamp_and_sign(g):
+            nc.vector.tensor_scalar(
+                out=size[g][:], in0=size[g][:], scalar1=2.0**-63, scalar2=2.0**63, op0=ALU.max, op1=ALU.min
+            )
+            nc.vector.tensor_scalar(
+                out=mask_sb[g][:], in0=mask_sb[g][:], scalar1=0.0, scalar2=0.5, op0=ALU.is_gt, op1=ALU.subtract
+            )
+
+        def logarithm(g):
+            nc.scalar.activation(out=recip[g][:], in_=size[g][:], func=ACT.Ln)
+
+        def inverse_magnitude(g):
+            nc.scalar.activation(out=recip[g][:], in_=recip[g][:], func=ACT.Exp, scale=-1.0)
+
+        def signed_inverse(g):
+            nc.vector.tensor_tensor(out=recip[g][:], in0=recip[g][:], in1=mask_sb[g][:], op=ALU.mult)
+
+        def logits(h, g):
+            s = live[("s", h, g)]
+            for j in range(PACK):
+                col = (2 * h + g) * PACK + j
+                nc.vector.scalar_tensor_tensor(
+                    out=s[:, j, :],
+                    in0=s[:, j, :],
+                    scalar=shift[:, col : col + 1],
+                    in1=recip[g][:, SKV * j : SKV * (j + 1)],
+                    op0=ALU.subtract,
+                    op1=ALU.subtract,
+                )
+
+        def exponential(h, g):
+            s = live[("s", h, g)]
+            p = flow.tile([P, SKV * PACK], BF16, name="p", tag="p", bufs=2, align_bytes=64)
+            nc.scalar.activation(
+                out=p[:].rearrange("p (c i j) -> p c j i", i=4, j=PACK),
+                in_=s[:].rearrange("p j (c i) -> p c j i", i=4),
+                func=ACT.Exp,
+            )
+            live[("p", h, g)] = p
+
+        def quantize_p(h, g):
+            p_mx = mx_tiles(flow, "p", SKV, 3)
+            quantize(p_mx, slice(0, SKV), E4, live[("p", h, g)][:])
+            live[("p_mx", h, g)] = p_mx
+
+        def grouped_tile(key):
+            if key not in live:
+                live[key] = flow.tile([P, 4096], BF16, name="grouped", tag="grouped", bufs=3, align_bytes=64)
+            return live[key]
+
+        def interleave_g(f, g, a, engine):
+            raw = live[("g", f, g)]
+            dst = grouped_tile(("gg", f, g))[:].rearrange("p (h s a m j) -> p a h m j s", h=2, s=4, a=2, j=PACK)
+            copy(engine, dst[:, 1 - a], raw[:, :, N * a : N * (a + 1)].rearrange("p j (m h s) -> p h m j s", h=2, s=4))
+
+        def zone(f, g, s):
+            return ((2 * f + g) * SLOTS + s) * ZONE
+
+        def quantize_g(f, g):
+            src = live[("gg", f, g)]
+            for s in range(SLOTS):
+                first = zone(f, g, s) + HALF
+                quantize(g_mx, slice(first, first + P), E5, src[:, N * s : N * (s + 1)])
+
+        def dxv_passes(h, g):
+            f, a = divmod(h, 2)
+            if a == 0 and g == 0:
+                live[("acc", f)] = [bank(4 * f + t) for t in range(PACK)]
+            for s in range(SLOTS):
+                t, e = divmod(s, 2)
+                first = zone(f, g, s) + (P if a == 0 else 0)
+                product(
+                    live[("acc", f)][t],
+                    g_mx, slice(first, first + P), E5,
+                    live[("p_mx", h, g)], slice(0, SKV), E4,
+                    start=(a == 0 and g == 0 and e == 0),
+                    stop=(a == 1 and g == 1 and e == 1),
+                )
+
+        def interleave_kv(c, part, engine):
+            raw = live[("kv", c)]
+            dst = grouped_tile(("kvg", c))[:, 2048 * part : 2048 * (part + 1)]
+            copy(
+                engine,
+                dst.rearrange("p (c i j) -> p c j i", i=4, j=PACK),
+                raw[:, :, N * part : N * (part + 1)].rearrange("p j (c i) -> p c j i", i=4),
+            )
+
+        def quantize_kv(c):
+            quantize(kv_mx[c], slice(0, 1024), E4, live[("kvg", c)][:])
+
+        def turn(words, firsts, k):
+            turned = bank(k)
+            for rr in range(2):
+                for u in range(2):
+                    nc.tensor.transpose(
+                        turned[:, P * (2 * rr + u) : P * (2 * rr + u + 1)],
+                        words[:, firsts[rr] + u : firsts[rr] + 2 * P : 2],
+                        ident[:],
+                    )
+            return turned
+
+        def collect(turned, dst, rp, engine):
+            view = dst.bitcast(F32).rearrange("p (m r u) -> p m r u", r=PACK, u=2)
+            copy(engine, view[:, :, 2 * rp : 2 * rp + 2, :], turned[:].rearrange("p (r u m) -> p m r u", r=2, u=2))
+
+        def turn_w(n, f, banks):
+            words = live[("w", n)][:].rearrange("p r c -> p (r c)").bitcast(F32)
+            for rp in range(2):
+                live[("wt", n, f, rp)] = turn(words, [N * (2 * rp + rr) + 2 * P * f for rr in range(2)], banks[rp])
+
+        def collect_w(n, f, engines):
+            dst = grouped_tile(("wg", n))[:, 2048 * f : 2048 * (f + 1)]
+            for rp in range(2):
+                collect(live[("wt", n, f, rp)], dst, rp, engines[rp])
+
+        def quantize_w(n):
+            quantize(w_mx[n], slice(0, 1024), E4, live[("wg", n)][:])
+
+        def round_dxv(f, engines):
+            d = flow.tile([P, PACK * SKV], BF16, name="d", tag="d", bufs=1, align_bytes=64)
+            for t in range(PACK):
+                copy(engines[t], d[:, SKV * t : SKV * (t + 1)], live[("acc", f)][t][:])
+            live[("d", f)] = d
+
+        def turn_dxv(f, banks):
+            words = live[("d", f)][:].bitcast(F32)
+            for rp in range(2):
+                live[("dt", f, rp)] = turn(words, [2 * P * (2 * rp + rr) for rr in range(2)], banks[rp])
+
+        def collect_dxv(f, engines):
+            dk = flow.tile([P, N * PACK], BF16, name="dk", tag="dk", bufs=1, align_bytes=64)
+            for rp in range(2):
+                collect(live[("dt", f, rp)], dk[:], rp, engines[rp])
+            live[("dk", f)] = dk
+
+        def interleave_dxv(f):
+            df = flow.tile([P, SKV * PACK], BF16, name="df", tag="df", bufs=1, align_bytes=64)
+            nc.vector.tensor_copy(
+                out=df[:].rearrange("p (c i t) -> p c t i", i=4, t=PACK),
+                in_=live[("d", f)][:].rearrange("p (t c i) -> p c t i", i=4, t=PACK),
+            )
+            live[("df", f)] = df
+
+        def quantize_dk(f):
+            quantize(dk_mx[f], slice(0, N), E5, live[("dk", f)][:])
+
+        def quantize_df(f):
+            quantize(df_mx[f], slice(0, N), E5, live[("df", f)][:])
+
+        def out_1_products(f, q, banks):
+            accs = [bank(k) for k in banks]
+            for r in range(2):
+                c, i = divmod(2 * q + r, 8)
+                product(accs[r], kv_mx[c], slice(P * i, P * (i + 1)), E4, dk_mx[f], slice(0, N), E5, True, True)
+            done.append((accs, out_1[2 * P * q : 2 * P * (q + 1), N * f : N * (f + 1)]))
+
+        def out_0_products(n, q, banks):
+            accs = [bank(k) for k in banks]
+            for r in range(2):
+                i = 2 * q + r
+                for f in range(2):
+                    product(
+                        accs[r],
+                        df_mx[f], slice(P * i, P * (i + 1)), E5,
+                        w_mx[n], slice(N * f, N * (f + 1)), E4,
+                        f == 0, f == 1,
+                    )
+            done.append((accs, out_0[0, 2 * P * q : 2 * P * (q + 1), N * n : N * (n + 1)]))
+
+        def store(engines):
+            accs, dst = done.pop(0)
+            stage = flow.tile([P, 2, N], F32, name="stage", tag="stage", bufs=6)
+            for r in range(2):
+                copy(engines[r], stage[:, r, :], accs[r][:])
+            nc.sync.dma_start(out=dst.rearrange("(r p) c -> p r c", p=P), in_=stage[:])
+
+        S, V = nc.scalar, nc.vector
+
+        load_mask(0)
+        load_g_half(0, 0, 0)
+        load_mask(1)
+        load_g_half(0, 0, 1)
+        load_g(0, 1)
+        nc.sync.dma_start(out=lse_sb[:], in_=lse[0].rearrange("h (g p j) -> p (h g) j", g=2, j=PACK))
+        load_scores(0, 0)
+        load_g(1, 0)
+        load_scores(0, 1)
+        load_scores(1, 0)
+        load_w(0)
+        load_g(1, 1)
+        nc.vector.memset(warm[:], 1.0)
+        nc.scalar.activation(out=warm[:], in_=warm[:], func=ACT.Ln)
+        nc.vector.memset(g_mx[0][:].rearrange("p (z c) -> p z c", c=ZONE)[:, :, 0:HALF], 0)
+        nc.vector.memset(g_mx[1][:].bitcast(U32).rearrange("p (z c) -> p z c", c=ZONE // 4)[:, :, 0 : HALF // 4], 0)
+        make_identity(nc, ident[:])
+
+        for g in range(2):
+            interleave_g(0, 0, g, V)
+            magnitude(g)
+            clamp_and_sign(g)
+        load_kv(0)
+        for g in range(2):
+            logarithm(g)
+        for g in range(2):
+            inverse_magnitude(g)
+        quantize_g(0, 0)
+        interleave_g(0, 1, 0, V)
+        interleave_g(0, 1, 1, V)
+        load_kv(1)
+        nc.vector.tensor_scalar(
+            out=shift[:], in0=lse_sb[:].rearrange("p c j -> p (c j)"), scalar1=1.0, scalar2=None, op0=ALU.subtract
+        )
+        quantize_g(0, 1)
+        interleave_g(1, 0, 1, V)
+        signed_inverse(0)
+
+        interleave_g(1, 0, 0, S)
+        load_w(1)
+        logits(0, 0)
+        signed_inverse(1)
+        exponential(0, 0)
+        load_scores(1, 1)
+        turn_w(0, 0, [4, 5])
+        turn_w(0, 1, [6, 7])
+        logits(0, 1)
+        collect_w(0, 0, [S, S])
+        collect_w(0, 1, [S, S])
+        quantize_p(0, 0)
+        dxv_passes(0, 0)
+        exponential(0, 1)
+        load_scores(2, 0)
+        load_w(2)
+        turn_w(1, 0, [4, 5])
+        turn_w(1, 1, [6, 7])
+        logits(1, 0)
+        quantize_g(1, 0)
+        interleave_g(1, 1, 0, S)
+        quantize_p(0, 1)
+        dxv_passes(0, 1)
+        exponential(1, 0)
+        load_scores(2, 1)
+        quantize_w(0)
+        logits(1, 1)
+        interleave_g(1, 1, 1, V)
+        load_w(3)
+        quantize_p(1, 0)
+        dxv_passes(1, 0)
+        exponential(1, 1)
+        load_scores(3, 0)
+        logits(2, 0)
+        collect_w(1, 0, [S, S])
+        collect_w(1, 1, [S, S])
+        quantize_p(1, 1)
+        dxv_passes(1, 1)
+        interleave_kv(0, 0, V)
+
+
+        exponential(2, 0)
+        load_scores(3, 1)
+        interleave_kv(0, 1, V)
+        round_dxv(0, [S, S, S, S])
+        turn_dxv(0, [0, 1])
+        logits(2, 1)
+        quantize_kv(0)
+        quantize_p(2, 0)
+        dxv_passes(2, 0)
+        collect_dxv(0, [S, S])
+        exponential(2, 1)
+        quantize_g(1, 1)
+        quantize_dk(0)
+        out_1_products(0, 0, [2, 3])
+        out_1_products(0, 1, [0, 1])
+        logits(3, 0)
+        quantize_p(2, 1)
+        dxv_passes(2, 1)
+        store([S, S])
+        out_1_products(0, 2, [2, 3])
+        interleave_kv(1, 0, V)
+        store([S, S])
+        out_1_products(0, 3, [0, 1])
+        exponential(3, 0)
+        logits(3, 1)
+        interleave_kv(1, 1, V)
+        quantize_p(3, 0)
+        dxv_passes(3, 0)
+        exponential(3, 1)
+        quantize_kv(1)
+        store([V, V])
+        out_1_products(0, 4, [2, 3])
+        quantize_p(3, 1)
+        store([S, S])
+        out_1_products(0, 5, [0, 1])
+        dxv_passes(3, 1)
+        interleave_dxv(0)
+        store([S, S])
+        out_1_products(0, 6, [2, 3])
+        quantize_w(1)
+        store([S, S])
+        out_1_products(0, 7, [0, 1])
+        round_dxv(1, [V, S, V, S])
+        turn_dxv(1, [4, 5])
+        quantize_df(0)
+        store([S, S])
+        turn_w(2, 0, [6, 7])
+        collect_dxv(1, [V, V])
+        store([S, S])
+        quantize_dk(1)
+        out_1_products(1, 0, [2, 3])
+        out_1_products(1, 1, [0, 1])
+        interleave_dxv(1)
+        collect_w(2, 0, [S, S])
+        turn_w(2, 1, [4, 5])
+        store([S, V])
+        quantize_df(1)
+        out_1_products(1, 2, [6, 7])
+        store([S, V])
+        out_0_products(0, 0, [2, 3])
+        collect_w(2, 1, [S, V])
+        out_1_products(1, 3, [0, 1])
+        turn_w(3, 0, [4, 5])
+        store([S, S])
+        quantize_w(2)
+        store([S, V])
+        out_1_products(1, 4, [6, 7])
+        turn_w(3, 1, [2, 3])
+        store([S, V])
+        collect_w(3, 0, [S, V])
+        out_0_products(0, 1, [0, 1])
+        out_1_products(1, 5, [4, 5])
+        store([S, V])
+        collect_w(3, 1, [S, V])
+        out_0_products(1, 0, [6, 7])
+        store([S, S])
+        quantize_w(3)
+        out_1_products(1, 6, [2, 3])
+        store([S, V])
+        out_0_products(1, 1, [0, 1])
+        store([S, V])
+        out_1_products(1, 7, [4, 5])
+        store([S, V])
+        ring = [[6, 7], [2, 3], [0, 1], [4, 5]]
+        for k in range(4):
+            out_0_products(2 + k // 2, k % 2, ring[k])
+            store([S, V])
+        for k in range(2):
+            store([S, V])

@@ -65,7 +65,9 @@ def tile_groupedqueryattention_pa_v_kernel(tc, xq, xk_rep, kv, mask, Wv, scores,
         lse_sb = keep.tile([P, 2 * HEADS, PACK], F32, name="lse_sb")
         shift = keep.tile([P, 2 * HEADS * PACK], F32, name="shift")
         mask_sb = [keep.tile([P, PACK * SKV], BF16, name="mask%d" % g) for g in range(2)]
-        size = [flow.tile([P, PACK * SKV], BF16, name="size%d" % g, tag="p", bufs=2, align_bytes=64) for g in range(2)]
+        spare = [flow.tile([P, PACK * SKV], BF16, name="spare%d" % g, tag="p", bufs=2, align_bytes=64) for g in range(2)]
+        sign = [spare[0], mask_sb[1]]
+        size = [mask_sb[0], spare[1]]
         recip = [keep.tile([P, PACK * SKV], F32, name="recip%d" % g) for g in range(2)]
         g_mx = mx_tiles(keep, "g", (4 * SLOTS + 1) * ZONE, 1)
         kv_mx = [mx_tiles(keep, "kv%d" % c, 1024, 1) for c in range(2)]
@@ -108,15 +110,14 @@ def tile_groupedqueryattention_pa_v_kernel(tc, xq, xk_rep, kv, mask, Wv, scores,
             nc.sync.dma_start(out=s[:], in_=scores[0, h, N * g : N * (g + 1), :].rearrange("(p j) k -> p j k", j=PACK))
             live[("s", h, g)] = s
 
-        def magnitude(g):
-            nc.scalar.activation(out=size[g][:], in_=mask_sb[g][:], func=ACT.Abs, scale=0.5)
+        def half_sign(g):
+            nc.vector.tensor_scalar(
+                out=sign[g][:], in0=mask_sb[g][:], scalar1=0.0, scalar2=0.5, op0=ALU.is_gt, op1=ALU.subtract
+            )
 
-        def clamp_and_sign(g):
+        def clamp(g):
             nc.vector.tensor_scalar(
                 out=size[g][:], in0=size[g][:], scalar1=2.0**-63, scalar2=2.0**63, op0=ALU.max, op1=ALU.min
-            )
-            nc.vector.tensor_scalar(
-                out=mask_sb[g][:], in0=mask_sb[g][:], scalar1=0.0, scalar2=0.5, op0=ALU.is_gt, op1=ALU.subtract
             )
 
         def logarithm(g):
@@ -126,7 +127,7 @@ def tile_groupedqueryattention_pa_v_kernel(tc, xq, xk_rep, kv, mask, Wv, scores,
             nc.scalar.activation(out=recip[g][:], in_=recip[g][:], func=ACT.Exp, scale=-1.0)
 
         def signed_inverse(g):
-            nc.vector.tensor_tensor(out=recip[g][:], in0=recip[g][:], in1=mask_sb[g][:], op=ALU.mult)
+            nc.vector.tensor_tensor(out=recip[g][:], in0=recip[g][:], in1=sign[g][:], op=ALU.mult)
 
         def logits(h, g):
             s = live[("s", h, g)]
@@ -266,33 +267,32 @@ def tile_groupedqueryattention_pa_v_kernel(tc, xq, xk_rep, kv, mask, Wv, scores,
             for r in range(2):
                 c, i = divmod(2 * q + r, 8)
                 product(accs[r], kv_mx[c], slice(P * i, P * (i + 1)), E4, dk_mx[f], slice(0, N), E5, True, True)
-            done.append((accs, out_1[2 * P * q : 2 * P * (q + 1), N * f : N * (f + 1)]))
+            done.append((accs, out_1[2 * P * q : 2 * P * (q + 1), N * f : N * (f + 1)].rearrange("(r p) c -> p r c", p=P)))
 
-        def out_0_products(n, q, banks):
+        def out_0_products(i, half, banks):
             accs = [bank(k) for k in banks]
             for r in range(2):
-                i = 2 * q + r
                 for f in range(2):
                     product(
                         accs[r],
                         df_mx[f], slice(P * i, P * (i + 1)), E5,
-                        w_mx[n], slice(N * f, N * (f + 1)), E4,
+                        w_mx[2 * half + r], slice(N * f, N * (f + 1)), E4,
                         f == 0, f == 1,
                     )
-            done.append((accs, out_0[0, 2 * P * q : 2 * P * (q + 1), N * n : N * (n + 1)]))
+            done.append((accs, out_0[0, P * i : P * (i + 1), 2 * N * half : 2 * N * (half + 1)].rearrange("p (r c) -> p r c", r=2)))
 
         def store(engines):
             accs, dst = done.pop(0)
             stage = flow.tile([P, 2, N], F32, name="stage", tag="stage", bufs=6)
             for r in range(2):
                 copy(engines[r], stage[:, r, :], accs[r][:])
-            nc.sync.dma_start(out=dst.rearrange("(r p) c -> p r c", p=P), in_=stage[:])
+            nc.sync.dma_start(out=dst, in_=stage[:])
 
         S, V = nc.scalar, nc.vector
 
         load_mask(0)
-        load_g_half(0, 0, 0)
         load_mask(1)
+        load_g_half(0, 0, 0)
         load_g_half(0, 0, 1)
         load_g(0, 1)
         nc.sync.dma_start(out=lse_sb[:], in_=lse[0].rearrange("h (g p j) -> p (h g) j", g=2, j=PACK))
@@ -300,18 +300,22 @@ def tile_groupedqueryattention_pa_v_kernel(tc, xq, xk_rep, kv, mask, Wv, scores,
         load_g(1, 0)
         load_scores(0, 1)
         load_scores(1, 0)
-        load_w(0)
         load_g(1, 1)
+        load_w(0)
         nc.vector.memset(warm[:], 1.0)
         nc.scalar.activation(out=warm[:], in_=warm[:], func=ACT.Ln)
         nc.vector.memset(g_mx[0][:].rearrange("p (z c) -> p z c", c=ZONE)[:, :, 0:HALF], 0)
         nc.vector.memset(g_mx[1][:].bitcast(U32).rearrange("p (z c) -> p z c", c=ZONE // 4)[:, :, 0 : HALF // 4], 0)
         make_identity(nc, ident[:])
 
-        for g in range(2):
-            interleave_g(0, 0, g, V)
-            magnitude(g)
-            clamp_and_sign(g)
+        half_sign(0)
+        nc.vector.tensor_tensor(out=size[0][:], in0=mask_sb[0][:], in1=sign[0][:], op=ALU.mult)
+        clamp(0)
+        nc.scalar.activation(out=size[1][:], in_=mask_sb[1][:], func=ACT.Abs, scale=0.5)
+        interleave_g(0, 0, 0, V)
+        clamp(1)
+        half_sign(1)
+        interleave_g(0, 0, 1, V)
         load_kv(0)
         for g in range(2):
             logarithm(g)
@@ -320,141 +324,139 @@ def tile_groupedqueryattention_pa_v_kernel(tc, xq, xk_rep, kv, mask, Wv, scores,
         quantize_g(0, 0)
         interleave_g(0, 1, 0, V)
         interleave_g(0, 1, 1, V)
-        load_kv(1)
         nc.vector.tensor_scalar(
             out=shift[:], in0=lse_sb[:].rearrange("p c j -> p (c j)"), scalar1=1.0, scalar2=None, op0=ALU.subtract
         )
         quantize_g(0, 1)
-        interleave_g(1, 0, 1, V)
         signed_inverse(0)
 
         interleave_g(1, 0, 0, S)
-        load_w(1)
         logits(0, 0)
         signed_inverse(1)
         exponential(0, 0)
         load_scores(1, 1)
+        load_w(1)
         turn_w(0, 0, [4, 5])
         turn_w(0, 1, [6, 7])
+        interleave_g(1, 0, 1, V)
         logits(0, 1)
-        collect_w(0, 0, [S, S])
-        collect_w(0, 1, [S, S])
+        interleave_g(1, 1, 0, S)
         quantize_p(0, 0)
         dxv_passes(0, 0)
         exponential(0, 1)
         load_scores(2, 0)
-        load_w(2)
-        turn_w(1, 0, [4, 5])
-        turn_w(1, 1, [6, 7])
         logits(1, 0)
         quantize_g(1, 0)
-        interleave_g(1, 1, 0, S)
+        collect_w(0, 0, [S, S])
+        collect_w(0, 1, [S, S])
         quantize_p(0, 1)
         dxv_passes(0, 1)
         exponential(1, 0)
         load_scores(2, 1)
-        quantize_w(0)
+        load_kv(1)
+        turn_w(1, 0, [4, 5])
+        turn_w(1, 1, [6, 7])
         logits(1, 1)
         interleave_g(1, 1, 1, V)
-        load_w(3)
         quantize_p(1, 0)
         dxv_passes(1, 0)
         exponential(1, 1)
         load_scores(3, 0)
+        load_w(2)
+        quantize_g(1, 1)
         logits(2, 0)
         collect_w(1, 0, [S, S])
         collect_w(1, 1, [S, S])
         quantize_p(1, 1)
         dxv_passes(1, 1)
-        interleave_kv(0, 0, V)
-
+        quantize_w(0)
 
         exponential(2, 0)
         load_scores(3, 1)
-        interleave_kv(0, 1, V)
+        load_w(3)
+        interleave_kv(0, 0, V)
         round_dxv(0, [S, S, S, S])
         turn_dxv(0, [0, 1])
         logits(2, 1)
-        quantize_kv(0)
         quantize_p(2, 0)
         dxv_passes(2, 0)
         collect_dxv(0, [S, S])
         exponential(2, 1)
-        quantize_g(1, 1)
+        interleave_kv(0, 1, V)
+        logits(3, 0)
+        interleave_kv(1, 0, S)
         quantize_dk(0)
+        quantize_kv(0)
         out_1_products(0, 0, [2, 3])
         out_1_products(0, 1, [0, 1])
-        logits(3, 0)
         quantize_p(2, 1)
         dxv_passes(2, 1)
-        store([S, S])
-        out_1_products(0, 2, [2, 3])
-        interleave_kv(1, 0, V)
-        store([S, S])
-        out_1_products(0, 3, [0, 1])
         exponential(3, 0)
         logits(3, 1)
-        interleave_kv(1, 1, V)
+        store([V, V])
+        out_1_products(0, 2, [2, 3])
         quantize_p(3, 0)
         dxv_passes(3, 0)
         exponential(3, 1)
-        quantize_kv(1)
         store([V, V])
-        out_1_products(0, 4, [2, 3])
+        out_1_products(0, 3, [0, 1])
+        interleave_kv(1, 1, V)
         quantize_p(3, 1)
-        store([S, S])
-        out_1_products(0, 5, [0, 1])
         dxv_passes(3, 1)
+        store([S, S])
+        quantize_kv(1)
+        store([S, S])
+        out_1_products(0, 4, [2, 3])
+        out_1_products(0, 5, [0, 1])
         interleave_dxv(0)
-        store([S, S])
-        out_1_products(0, 6, [2, 3])
-        quantize_w(1)
-        store([S, S])
-        out_1_products(0, 7, [0, 1])
-        round_dxv(1, [V, S, V, S])
+        round_dxv(1, [S, S, V, V])
         turn_dxv(1, [4, 5])
-        quantize_df(0)
         store([S, S])
-        turn_w(2, 0, [6, 7])
+        out_1_products(0, 6, [6, 7])
+        out_1_products(0, 7, [2, 3])
         collect_dxv(1, [V, V])
         store([S, S])
+        turn_w(2, 0, [0, 1])
+        quantize_df(0)
         quantize_dk(1)
-        out_1_products(1, 0, [2, 3])
-        out_1_products(1, 1, [0, 1])
+        store([S, S])
+        out_1_products(1, 0, [4, 5])
+        out_1_products(1, 1, [6, 7])
+        quantize_w(1)
+        store([S, S])
         interleave_dxv(1)
-        collect_w(2, 0, [S, S])
+        out_1_products(1, 2, [2, 3])
+        store([S, S])
         turn_w(2, 1, [4, 5])
-        store([S, V])
+        collect_w(2, 0, [V, V])
         quantize_df(1)
-        out_1_products(1, 2, [6, 7])
-        store([S, V])
-        out_0_products(0, 0, [2, 3])
-        collect_w(2, 1, [S, V])
+        store([S, S])
         out_1_products(1, 3, [0, 1])
-        turn_w(3, 0, [4, 5])
+        out_0_products(0, 0, [6, 7])
+        store([S, V])
+        collect_w(2, 1, [S, V])
+        turn_w(3, 0, [2, 3])
         store([S, S])
         quantize_w(2)
-        store([S, V])
-        out_1_products(1, 4, [6, 7])
-        turn_w(3, 1, [2, 3])
+        out_1_products(1, 4, [4, 5])
+        turn_w(3, 1, [0, 1])
         store([S, V])
         collect_w(3, 0, [S, V])
-        out_0_products(0, 1, [0, 1])
-        out_1_products(1, 5, [4, 5])
+        out_1_products(1, 5, [6, 7])
+        out_0_products(1, 0, [2, 3])
         store([S, V])
         collect_w(3, 1, [S, V])
-        out_0_products(1, 0, [6, 7])
+        out_1_products(1, 6, [4, 5])
+        out_0_products(2, 0, [0, 1])
         store([S, S])
         quantize_w(3)
-        out_1_products(1, 6, [2, 3])
         store([S, V])
-        out_0_products(1, 1, [0, 1])
+        out_1_products(1, 7, [6, 7])
+        out_0_products(3, 0, [2, 3])
         store([S, V])
-        out_1_products(1, 7, [4, 5])
-        store([S, V])
-        ring = [[6, 7], [2, 3], [0, 1], [4, 5]]
-        for k in range(4):
-            out_0_products(2 + k // 2, k % 2, ring[k])
+        ring = [[4, 5], [0, 1], [6, 7], [2, 3]]
+        for i in range(4):
+            out_0_products(i, 1, ring[i])
             store([S, V])
-        for k in range(2):
+        for k in range(3):
             store([S, V])

@@ -84,7 +84,7 @@ def tile_groupedqueryattention_pa_v_kernel(tc, xq, xk_rep, kv, mask, Wv, scores,
             )
 
         def load_rows(key, rows):
-            raw = flow.tile([P, PACK, 1024], BF16, name="raw", tag="raw", bufs=5)
+            raw = flow.tile([P, PACK, 1024], BF16, name="raw", tag="raw", bufs=5, align_bytes=64)
             nc.sync.dma_start(out=raw[:], in_=rows.rearrange("(p j) c -> p j c", j=PACK))
             live[key] = raw
 
@@ -93,7 +93,7 @@ def tile_groupedqueryattention_pa_v_kernel(tc, xq, xk_rep, kv, mask, Wv, scores,
 
         def load_g_half(f, g, a):
             if a == 0:
-                live[("g", f, g)] = flow.tile([P, PACK, 1024], BF16, name="raw", tag="raw", bufs=5)
+                live[("g", f, g)] = flow.tile([P, PACK, 1024], BF16, name="raw", tag="raw", bufs=5, align_bytes=64)
             rows = grad_out[0, N * g : N * (g + 1), 1024 * f + N * a : 1024 * f + N * (a + 1)]
             nc.sync.dma_start(
                 out=live[("g", f, g)][:, :, N * a : N * (a + 1)], in_=rows.rearrange("(p j) c -> p j c", j=PACK)
@@ -123,11 +123,11 @@ def tile_groupedqueryattention_pa_v_kernel(tc, xq, xk_rep, kv, mask, Wv, scores,
         def logarithm(g):
             nc.scalar.activation(out=recip[g][:], in_=size[g][:], func=ACT.Ln)
 
-        def inverse_magnitude(g):
-            nc.scalar.activation(out=recip[g][:], in_=recip[g][:], func=ACT.Exp, scale=-1.0)
+        def inverse_magnitude(g, cols):
+            nc.scalar.activation(out=recip[g][:, cols], in_=recip[g][:, cols], func=ACT.Exp, scale=-1.0)
 
-        def signed_inverse(g):
-            nc.vector.tensor_tensor(out=recip[g][:], in0=recip[g][:], in1=sign[g][:], op=ALU.mult)
+        def signed_inverse(g, cols):
+            nc.vector.tensor_tensor(out=recip[g][:, cols], in0=recip[g][:, cols], in1=sign[g][:, cols], op=ALU.mult)
 
         def logits(h, g):
             s = live[("s", h, g)]
@@ -224,6 +224,9 @@ def tile_groupedqueryattention_pa_v_kernel(tc, xq, xk_rep, kv, mask, Wv, scores,
                 live[("wt", n, f, rp)] = turn(words, [N * (2 * rp + rr) + 2 * P * f for rr in range(2)], banks[rp])
 
         def collect_w(n, f, engines):
+            if n < 2 and f == 0:
+                held = flow.tile([P, PACK, 1024], BF16, name="held", tag="raw", bufs=5, align_bytes=64)
+                live[("wg", n)] = held[:].rearrange("p r c -> p (r c)")
             dst = grouped_tile(("wg", n))[:, 2048 * f : 2048 * (f + 1)]
             for rp in range(2):
                 collect(live[("wt", n, f, rp)], dst, rp, engines[rp])
@@ -319,30 +322,33 @@ def tile_groupedqueryattention_pa_v_kernel(tc, xq, xk_rep, kv, mask, Wv, scores,
         load_kv(0)
         for g in range(2):
             logarithm(g)
-        for g in range(2):
-            inverse_magnitude(g)
-        quantize_g(0, 0)
+        halves = [slice(0, 1024), slice(1024, 2048)]
+        for cols in halves:
+            inverse_magnitude(0, cols)
+        inverse_magnitude(1, slice(0, 2048))
         interleave_g(0, 1, 0, V)
+        quantize_g(0, 0)
         interleave_g(0, 1, 1, V)
         nc.vector.tensor_scalar(
             out=shift[:], in0=lse_sb[:].rearrange("p c j -> p (c j)"), scalar1=1.0, scalar2=None, op0=ALU.subtract
         )
-        quantize_g(0, 1)
-        signed_inverse(0)
+        for cols in halves:
+            signed_inverse(0, cols)
 
         interleave_g(1, 0, 0, S)
         logits(0, 0)
-        signed_inverse(1)
+        signed_inverse(1, slice(0, 2048))
         exponential(0, 0)
         load_scores(1, 1)
         load_w(1)
         turn_w(0, 0, [4, 5])
         turn_w(0, 1, [6, 7])
-        interleave_g(1, 0, 1, V)
+        quantize_g(0, 1)
         logits(0, 1)
-        interleave_g(1, 1, 0, S)
         quantize_p(0, 0)
         dxv_passes(0, 0)
+        interleave_g(1, 1, 0, S)
+        interleave_g(1, 0, 1, V)
         exponential(0, 1)
         load_scores(2, 0)
         logits(1, 0)
@@ -353,110 +359,109 @@ def tile_groupedqueryattention_pa_v_kernel(tc, xq, xk_rep, kv, mask, Wv, scores,
         dxv_passes(0, 1)
         exponential(1, 0)
         load_scores(2, 1)
-        load_kv(1)
         turn_w(1, 0, [4, 5])
         turn_w(1, 1, [6, 7])
         logits(1, 1)
         interleave_g(1, 1, 1, V)
+        load_kv(1)
         quantize_p(1, 0)
         dxv_passes(1, 0)
         exponential(1, 1)
         load_scores(3, 0)
-        load_w(2)
-        quantize_g(1, 1)
+        interleave_kv(0, 0, V)
         logits(2, 0)
         collect_w(1, 0, [S, S])
         collect_w(1, 1, [S, S])
         quantize_p(1, 1)
         dxv_passes(1, 1)
-        quantize_w(0)
+        interleave_kv(0, 1, V)
 
         exponential(2, 0)
         load_scores(3, 1)
+        load_w(2)
         load_w(3)
-        interleave_kv(0, 0, V)
         round_dxv(0, [S, S, S, S])
         turn_dxv(0, [0, 1])
         logits(2, 1)
         quantize_p(2, 0)
         dxv_passes(2, 0)
         collect_dxv(0, [S, S])
-        exponential(2, 1)
-        interleave_kv(0, 1, V)
-        logits(3, 0)
-        interleave_kv(1, 0, S)
-        quantize_dk(0)
         quantize_kv(0)
+        exponential(2, 1)
+        quantize_g(1, 1)
+        quantize_dk(0)
         out_1_products(0, 0, [2, 3])
         out_1_products(0, 1, [0, 1])
+        logits(3, 0)
+        store([S, S])
+        out_1_products(0, 2, [2, 3])
         quantize_p(2, 1)
         dxv_passes(2, 1)
+        store([S, S])
+        out_1_products(0, 3, [0, 1])
         exponential(3, 0)
         logits(3, 1)
-        store([V, V])
-        out_1_products(0, 2, [2, 3])
+        interleave_kv(1, 0, V)
         quantize_p(3, 0)
         dxv_passes(3, 0)
         exponential(3, 1)
-        store([V, V])
-        out_1_products(0, 3, [0, 1])
         interleave_kv(1, 1, V)
         quantize_p(3, 1)
         dxv_passes(3, 1)
-        store([S, S])
         quantize_kv(1)
+        store([S, S])
         store([S, S])
         out_1_products(0, 4, [2, 3])
         out_1_products(0, 5, [0, 1])
         interleave_dxv(0)
         round_dxv(1, [S, S, V, V])
         turn_dxv(1, [4, 5])
-        store([S, S])
         out_1_products(0, 6, [6, 7])
+        store([S, V])
         out_1_products(0, 7, [2, 3])
-        collect_dxv(1, [V, V])
-        store([S, S])
+        store([S, V])
+        collect_dxv(1, [S, V])
         turn_w(2, 0, [0, 1])
-        quantize_df(0)
-        quantize_dk(1)
         store([S, S])
+        quantize_dk(1)
         out_1_products(1, 0, [4, 5])
         out_1_products(1, 1, [6, 7])
+        quantize_df(0)
+        store([S, S])
+        out_1_products(1, 2, [2, 3])
+        interleave_dxv(1)
+        store([S, S])
+        out_1_products(1, 3, [4, 5])
+        quantize_w(0)
+        store([S, S])
+        turn_w(2, 1, [6, 7])
+        quantize_df(1)
         quantize_w(1)
         store([S, S])
-        interleave_dxv(1)
-        out_1_products(1, 2, [2, 3])
-        store([S, S])
-        turn_w(2, 1, [4, 5])
+        out_1_products(1, 4, [2, 3])
         collect_w(2, 0, [V, V])
-        quantize_df(1)
         store([S, S])
-        out_1_products(1, 3, [0, 1])
-        out_0_products(0, 0, [6, 7])
-        store([S, V])
-        collect_w(2, 1, [S, V])
-        turn_w(3, 0, [2, 3])
+        out_1_products(1, 5, [4, 5])
+        turn_w(3, 0, [0, 1])
+        collect_w(2, 1, [V, V])
         store([S, S])
+        out_1_products(1, 6, [2, 3])
+        turn_w(3, 1, [6, 7])
         quantize_w(2)
-        out_1_products(1, 4, [4, 5])
-        turn_w(3, 1, [0, 1])
-        store([S, V])
-        collect_w(3, 0, [S, V])
-        out_1_products(1, 5, [6, 7])
-        out_0_products(1, 0, [2, 3])
-        store([S, V])
-        collect_w(3, 1, [S, V])
-        out_1_products(1, 6, [4, 5])
-        out_0_products(2, 0, [0, 1])
         store([S, S])
+        out_1_products(1, 7, [4, 5])
+        collect_w(3, 0, [V, V])
+        store([S, S])
+        out_0_products(0, 0, [2, 3])
+        collect_w(3, 1, [V, V])
+        out_0_products(1, 0, [0, 1])
+        store([S, S])
+        out_0_products(2, 0, [4, 5])
         quantize_w(3)
-        store([S, V])
-        out_1_products(1, 7, [6, 7])
-        out_0_products(3, 0, [2, 3])
-        store([S, V])
-        ring = [[4, 5], [0, 1], [6, 7], [2, 3]]
-        for i in range(4):
-            out_0_products(i, 1, ring[i])
+        store([S, S])
+        ring = [[6, 7], [2, 3], [0, 1], [4, 5]]
+        for k in range(5):
+            out_0_products((3 + k) % 4, min(k, 1), ring[k % 4])
             store([S, V])
-        for k in range(3):
+        for k in range(2):
             store([S, V])

from contextlib import ExitStack

import concourse.mybir as mybir
from concourse.masks import make_identity

SQ, SKV, DIN, HEADS, DIMS, FEATS = 1024, 512, 2048, 4, 2048, 1024
FLOPS = 2 * SQ * SKV * DIMS + 2 * 2 * SKV * DIN * FEATS
BYTES = 2 * (SKV * DIN + SQ * SKV + DIN * FEATS + SQ * DIMS) + 4 * (HEADS * SQ * SKV + HEADS * SQ + SKV * DIN + DIN * FEATS)

F32 = mybir.dt.float32
BF16 = mybir.dt.bfloat16
U32 = mybir.dt.uint32
U8 = mybir.dt.uint8
E4 = mybir.dt.float8_e4m3fn_x4
E5 = mybir.dt.float8_e5m2_x4
ACT = mybir.ActivationFunctionType
ALU = mybir.AluOpType

P = 128
PACK = 4
N = 512
HALF = 64
ZONE = 3 * HALF
SLOTS = 8


def tile_groupedqueryattention_pa_v_kernel(tc, xq, xk_rep, kv, mask, Wv, scores, lse, grad_out, out_0, out_1):
    nc = tc.nc
    with ExitStack() as ctx:
        keep = ctx.enter_context(tc.tile_pool(name="keep", bufs=1))
        flow = ctx.enter_context(tc.tile_pool(name="flow", bufs=2))
        psum = ctx.enter_context(tc.psum_pool(name="psum", bufs=1))
        ctx.enter_context(tc.manual_schedule())

        def copy(engine, out, in_):
            if engine is nc.scalar:
                nc.scalar.copy(out=out, in_=in_)
            else:
                nc.vector.tensor_copy(out=out, in_=in_)

        def bank(k):
            return psum.tile([P, N], F32, name="bank%d" % k, tag="bank%d" % k)

        def mx_tiles(pool, name, width, bufs):
            codes = pool.tile([P, width], U32, name=name + "_codes", tag=name + "_codes", bufs=bufs, align_bytes=64)
            scales = pool.tile([P, width], U8, name=name + "_scales", tag=name + "_scales", bufs=bufs, align_bytes=64)
            return codes, scales

        def quantize(mx, cols, fmt, values):
            nc.vector.quantize_mx(out=mx[0][:, cols].bitcast(fmt), scales=mx[1][:, cols], in_=values)

        def product(acc, lhs, lhs_cols, lhs_fmt, rhs, rhs_cols, rhs_fmt, start, stop):
            nc.tensor.matmul_mx(
                out=acc[:],
                lhsT=lhs[0][:, lhs_cols].bitcast(lhs_fmt),
                lhsT_scale=lhs[1][:, lhs_cols],
                rhs=rhs[0][:, rhs_cols].bitcast(rhs_fmt),
                rhs_scale=rhs[1][:, rhs_cols],
                start=start,
                stop=stop,
            )

        ident = keep.tile([P, P], F32, name="ident")
        warm = keep.tile([P, 1], F32, name="warm")
        lse_sb = keep.tile([P, 2 * HEADS, PACK], F32, name="lse_sb")
        shift = keep.tile([P, 2 * HEADS * PACK], F32, name="shift")
        mask_sb = [keep.tile([P, PACK * SKV], BF16, name="mask%d" % g) for g in range(2)]
        spare = [flow.tile([P, PACK * SKV], BF16, name="spare%d" % g, tag="p", bufs=2, align_bytes=64) for g in range(2)]
        sign = [spare[0], mask_sb[1]]
        size = [mask_sb[0], spare[1]]
        recip = [keep.tile([P, PACK * SKV], F32, name="recip%d" % g) for g in range(2)]
        g_mx = mx_tiles(keep, "g", (4 * SLOTS + 1) * ZONE, 1)
        kv_mx = [mx_tiles(keep, "kv%d" % c, 1024, 1) for c in range(2)]
        w_mx = [mx_tiles(keep, "w%d" % n, 1024, 1) for n in range(4)]
        df_mx = [mx_tiles(keep, "df%d" % f, N, 1) for f in range(2)]
        dk_mx = [mx_tiles(keep, "dk%d" % f, N, 1) for f in range(2)]
        live = {}
        done = []

        def load_mask(g):
            nc.sync.dma_start(
                out=mask_sb[g][:].rearrange("p (j k) -> p j k", j=PACK),
                in_=mask[0, 0, N * g : N * (g + 1), :].rearrange("(p j) k -> p j k", j=PACK),
            )

        def load_rows(key, rows):
            raw = flow.tile([P, PACK, 1024], BF16, name="raw", tag="raw", bufs=5, align_bytes=64)
            nc.sync.dma_start(out=raw[:], in_=rows.rearrange("(p j) c -> p j c", j=PACK))
            live[key] = raw

        def load_g(f, g):
            load_rows(("g", f, g), grad_out[0, N * g : N * (g + 1), 1024 * f : 1024 * (f + 1)])

        def load_g_half(f, g, a):
            if a == 0:
                live[("g", f, g)] = flow.tile([P, PACK, 1024], BF16, name="raw", tag="raw", bufs=5, align_bytes=64)
            rows = grad_out[0, N * g : N * (g + 1), 1024 * f + N * a : 1024 * f + N * (a + 1)]
            nc.sync.dma_start(
                out=live[("g", f, g)][:, :, N * a : N * (a + 1)], in_=rows.rearrange("(p j) c -> p j c", j=PACK)
            )

        def load_kv(c):
            load_rows(("kv", c), kv[0, :, 1024 * c : 1024 * (c + 1)])

        def load_w(n):
            load_rows(("w", n), Wv[N * n : N * (n + 1), :])

        def load_scores(h, g):
            s = flow.tile([P, PACK, SKV], F32, name="s", tag="s", bufs=3)
            nc.sync.dma_start(out=s[:], in_=scores[0, h, N * g : N * (g + 1), :].rearrange("(p j) k -> p j k", j=PACK))
            live[("s", h, g)] = s

        def half_sign(g):
            nc.vector.tensor_scalar(
                out=sign[g][:], in0=mask_sb[g][:], scalar1=0.0, scalar2=0.5, op0=ALU.is_gt, op1=ALU.subtract
            )

        def clamp(g):
            nc.vector.tensor_scalar(
                out=size[g][:], in0=size[g][:], scalar1=2.0**-63, scalar2=2.0**63, op0=ALU.max, op1=ALU.min
            )

        def logarithm(g):
            nc.scalar.activation(out=recip[g][:], in_=size[g][:], func=ACT.Ln)

        def inverse_magnitude(g, cols):
            nc.scalar.activation(out=recip[g][:, cols], in_=recip[g][:, cols], func=ACT.Exp, scale=-1.0)

        def signed_inverse(g, cols):
            nc.vector.tensor_tensor(out=recip[g][:, cols], in0=recip[g][:, cols], in1=sign[g][:, cols], op=ALU.mult)

        def logits(h, g):
            s = live[("s", h, g)]
            for j in range(PACK):
                col = (2 * h + g) * PACK + j
                nc.vector.scalar_tensor_tensor(
                    out=s[:, j, :],
                    in0=s[:, j, :],
                    scalar=shift[:, col : col + 1],
                    in1=recip[g][:, SKV * j : SKV * (j + 1)],
                    op0=ALU.subtract,
                    op1=ALU.subtract,
                )

        def exponential(h, g):
            s = live[("s", h, g)]
            p = flow.tile([P, SKV * PACK], BF16, name="p", tag="p", bufs=2, align_bytes=64)
            nc.scalar.activation(
                out=p[:].rearrange("p (c i j) -> p c j i", i=4, j=PACK),
                in_=s[:].rearrange("p j (c i) -> p c j i", i=4),
                func=ACT.Exp,
            )
            live[("p", h, g)] = p

        def quantize_p(h, g):
            p_mx = mx_tiles(flow, "p", SKV, 3)
            quantize(p_mx, slice(0, SKV), E4, live[("p", h, g)][:])
            live[("p_mx", h, g)] = p_mx

        def grouped_tile(key):
            if key not in live:
                live[key] = flow.tile([P, 4096], BF16, name="grouped", tag="grouped", bufs=3, align_bytes=64)
            return live[key]

        def interleave_g(f, g, a, engine):
            raw = live[("g", f, g)]
            dst = grouped_tile(("gg", f, g))[:].rearrange("p (h s a m j) -> p a h m j s", h=2, s=4, a=2, j=PACK)
            copy(engine, dst[:, 1 - a], raw[:, :, N * a : N * (a + 1)].rearrange("p j (m h s) -> p h m j s", h=2, s=4))

        def zone(f, g, s):
            return ((2 * f + g) * SLOTS + s) * ZONE

        def quantize_g(f, g):
            src = live[("gg", f, g)]
            for s in range(SLOTS):
                first = zone(f, g, s) + HALF
                quantize(g_mx, slice(first, first + P), E5, src[:, N * s : N * (s + 1)])

        def dxv_passes(h, g):
            f, a = divmod(h, 2)
            if a == 0 and g == 0:
                live[("acc", f)] = [bank(4 * f + t) for t in range(PACK)]
            for s in range(SLOTS):
                t, e = divmod(s, 2)
                first = zone(f, g, s) + (P if a == 0 else 0)
                product(
                    live[("acc", f)][t],
                    g_mx, slice(first, first + P), E5,
                    live[("p_mx", h, g)], slice(0, SKV), E4,
                    start=(a == 0 and g == 0 and e == 0),
                    stop=(a == 1 and g == 1 and e == 1),
                )

        def interleave_kv(c, part, engine):
            raw = live[("kv", c)]
            dst = grouped_tile(("kvg", c))[:, 2048 * part : 2048 * (part + 1)]
            copy(
                engine,
                dst.rearrange("p (c i j) -> p c j i", i=4, j=PACK),
                raw[:, :, N * part : N * (part + 1)].rearrange("p j (c i) -> p c j i", i=4),
            )

        def quantize_kv(c):
            quantize(kv_mx[c], slice(0, 1024), E4, live[("kvg", c)][:])

        def turn(words, firsts, k):
            turned = bank(k)
            for rr in range(2):
                for u in range(2):
                    nc.tensor.transpose(
                        turned[:, P * (2 * rr + u) : P * (2 * rr + u + 1)],
                        words[:, firsts[rr] + u : firsts[rr] + 2 * P : 2],
                        ident[:],
                    )
            return turned

        def collect(turned, dst, rp, engine):
            view = dst.bitcast(F32).rearrange("p (m r u) -> p m r u", r=PACK, u=2)
            copy(engine, view[:, :, 2 * rp : 2 * rp + 2, :], turned[:].rearrange("p (r u m) -> p m r u", r=2, u=2))

        def turn_w(n, f, banks):
            words = live[("w", n)][:].rearrange("p r c -> p (r c)").bitcast(F32)
            for rp in range(2):
                live[("wt", n, f, rp)] = turn(words, [N * (2 * rp + rr) + 2 * P * f for rr in range(2)], banks[rp])

        def collect_w(n, f, engines):
            if n < 2 and f == 0:
                held = flow.tile([P, PACK, 1024], BF16, name="held", tag="raw", bufs=5, align_bytes=64)
                live[("wg", n)] = held[:].rearrange("p r c -> p (r c)")
            dst = grouped_tile(("wg", n))[:, 2048 * f : 2048 * (f + 1)]
            for rp in range(2):
                collect(live[("wt", n, f, rp)], dst, rp, engines[rp])

        def quantize_w(n):
            quantize(w_mx[n], slice(0, 1024), E4, live[("wg", n)][:])

        def round_dxv(f, engines):
            d = flow.tile([P, PACK * SKV], BF16, name="d", tag="d", bufs=1, align_bytes=64)
            for t in range(PACK):
                copy(engines[t], d[:, SKV * t : SKV * (t + 1)], live[("acc", f)][t][:])
            live[("d", f)] = d

        def turn_dxv(f, banks):
            words = live[("d", f)][:].bitcast(F32)
            for rp in range(2):
                live[("dt", f, rp)] = turn(words, [2 * P * (2 * rp + rr) for rr in range(2)], banks[rp])

        def collect_dxv(f, engines):
            dk = flow.tile([P, N * PACK], BF16, name="dk", tag="dk", bufs=1, align_bytes=64)
            for rp in range(2):
                collect(live[("dt", f, rp)], dk[:], rp, engines[rp])
            live[("dk", f)] = dk

        def interleave_dxv(f):
            df = flow.tile([P, SKV * PACK], BF16, name="df", tag="df", bufs=1, align_bytes=64)
            nc.vector.tensor_copy(
                out=df[:].rearrange("p (c i t) -> p c t i", i=4, t=PACK),
                in_=live[("d", f)][:].rearrange("p (t c i) -> p c t i", i=4, t=PACK),
            )
            live[("df", f)] = df

        def quantize_dk(f):
            quantize(dk_mx[f], slice(0, N), E5, live[("dk", f)][:])

        def quantize_df(f):
            quantize(df_mx[f], slice(0, N), E5, live[("df", f)][:])

        def out_1_products(f, q, banks):
            accs = [bank(k) for k in banks]
            for r in range(2):
                c, i = divmod(2 * q + r, 8)
                product(accs[r], kv_mx[c], slice(P * i, P * (i + 1)), E4, dk_mx[f], slice(0, N), E5, True, True)
            done.append((accs, out_1[2 * P * q : 2 * P * (q + 1), N * f : N * (f + 1)].rearrange("(r p) c -> p r c", p=P)))

        def out_0_products(i, half, banks):
            accs = [bank(k) for k in banks]
            for r in range(2):
                for f in range(2):
                    product(
                        accs[r],
                        df_mx[f], slice(P * i, P * (i + 1)), E5,
                        w_mx[2 * half + r], slice(N * f, N * (f + 1)), E4,
                        f == 0, f == 1,
                    )
            done.append((accs, out_0[0, P * i : P * (i + 1), 2 * N * half : 2 * N * (half + 1)].rearrange("p (r c) -> p r c", r=2)))

        def store(engines):
            accs, dst = done.pop(0)
            stage = flow.tile([P, 2, N], F32, name="stage", tag="stage", bufs=6)
            for r in range(2):
                copy(engines[r], stage[:, r, :], accs[r][:])
            nc.sync.dma_start(out=dst, in_=stage[:])

        S, V = nc.scalar, nc.vector

        load_mask(0)
        load_mask(1)
        load_g_half(0, 0, 0)
        load_g_half(0, 0, 1)
        load_g(0, 1)
        nc.sync.dma_start(out=lse_sb[:], in_=lse[0].rearrange("h (g p j) -> p (h g) j", g=2, j=PACK))
        load_scores(0, 0)
        load_g(1, 0)
        load_scores(0, 1)
        load_scores(1, 0)
        load_g(1, 1)
        load_w(0)
        nc.vector.memset(warm[:], 1.0)
        nc.scalar.activation(out=warm[:], in_=warm[:], func=ACT.Ln)
        nc.vector.memset(g_mx[0][:].rearrange("p (z c) -> p z c", c=ZONE)[:, :, 0:HALF], 0)
        nc.vector.memset(g_mx[1][:].bitcast(U32).rearrange("p (z c) -> p z c", c=ZONE // 4)[:, :, 0 : HALF // 4], 0)
        make_identity(nc, ident[:])

        half_sign(0)
        nc.vector.tensor_tensor(out=size[0][:], in0=mask_sb[0][:], in1=sign[0][:], op=ALU.mult)
        clamp(0)
        nc.scalar.activation(out=size[1][:], in_=mask_sb[1][:], func=ACT.Abs, scale=0.5)
        interleave_g(0, 0, 0, V)
        clamp(1)
        half_sign(1)
        interleave_g(0, 0, 1, V)
        load_kv(0)
        for g in range(2):
            logarithm(g)
        halves = [slice(0, 1024), slice(1024, 2048)]
        for cols in halves:
            inverse_magnitude(0, cols)
        inverse_magnitude(1, slice(0, 2048))
        interleave_g(0, 1, 0, V)
        quantize_g(0, 0)
        interleave_g(0, 1, 1, V)
        nc.vector.tensor_scalar(
            out=shift[:], in0=lse_sb[:].rearrange("p c j -> p (c j)"), scalar1=1.0, scalar2=None, op0=ALU.subtract
        )
        for cols in halves:
            signed_inverse(0, cols)

        interleave_g(1, 0, 0, S)
        logits(0, 0)
        signed_inverse(1, slice(0, 2048))
        exponential(0, 0)
        load_scores(1, 1)
        load_w(1)
        turn_w(0, 0, [4, 5])
        turn_w(0, 1, [6, 7])
        quantize_g(0, 1)
        logits(0, 1)
        quantize_p(0, 0)
        dxv_passes(0, 0)
        interleave_g(1, 1, 0, S)
        interleave_g(1, 0, 1, V)
        exponential(0, 1)
        load_scores(2, 0)
        logits(1, 0)
        quantize_g(1, 0)
        collect_w(0, 0, [S, S])
        collect_w(0, 1, [S, S])
        quantize_p(0, 1)
        dxv_passes(0, 1)
        exponential(1, 0)
        load_scores(2, 1)
        turn_w(1, 0, [4, 5])
        turn_w(1, 1, [6, 7])
        logits(1, 1)
        interleave_g(1, 1, 1, V)
        load_kv(1)
        quantize_p(1, 0)
        dxv_passes(1, 0)
        exponential(1, 1)
        load_scores(3, 0)
        interleave_kv(0, 0, V)
        logits(2, 0)
        collect_w(1, 0, [S, S])
        collect_w(1, 1, [S, S])
        quantize_p(1, 1)
        dxv_passes(1, 1)
        interleave_kv(0, 1, V)

        exponential(2, 0)
        load_scores(3, 1)
        load_w(2)
        load_w(3)
        round_dxv(0, [S, S, S, S])
        turn_dxv(0, [0, 1])
        logits(2, 1)
        quantize_p(2, 0)
        dxv_passes(2, 0)
        collect_dxv(0, [S, S])
        quantize_kv(0)
        exponential(2, 1)
        quantize_g(1, 1)
        quantize_dk(0)
        out_1_products(0, 0, [2, 3])
        out_1_products(0, 1, [0, 1])
        logits(3, 0)
        store([S, S])
        out_1_products(0, 2, [2, 3])
        quantize_p(2, 1)
        dxv_passes(2, 1)
        store([S, S])
        out_1_products(0, 3, [0, 1])
        exponential(3, 0)
        logits(3, 1)
        interleave_kv(1, 0, V)
        quantize_p(3, 0)
        dxv_passes(3, 0)
        exponential(3, 1)
        interleave_kv(1, 1, V)
        quantize_p(3, 1)
        dxv_passes(3, 1)
        quantize_kv(1)
        store([S, S])
        store([S, S])
        out_1_products(0, 4, [2, 3])
        out_1_products(0, 5, [0, 1])
        interleave_dxv(0)
        round_dxv(1, [S, S, V, V])
        turn_dxv(1, [4, 5])
        out_1_products(0, 6, [6, 7])
        store([S, V])
        out_1_products(0, 7, [2, 3])
        store([S, V])
        collect_dxv(1, [S, V])
        turn_w(2, 0, [0, 1])
        store([S, S])
        quantize_dk(1)
        out_1_products(1, 0, [4, 5])
        out_1_products(1, 1, [6, 7])
        quantize_df(0)
        store([S, S])
        out_1_products(1, 2, [2, 3])
        interleave_dxv(1)
        store([S, S])
        out_1_products(1, 3, [4, 5])
        quantize_w(0)
        store([S, S])
        turn_w(2, 1, [6, 7])
        quantize_df(1)
        quantize_w(1)
        store([S, S])
        out_1_products(1, 4, [2, 3])
        collect_w(2, 0, [V, V])
        store([S, S])
        out_1_products(1, 5, [4, 5])
        turn_w(3, 0, [0, 1])
        collect_w(2, 1, [V, V])
        store([S, S])
        out_1_products(1, 6, [2, 3])
        turn_w(3, 1, [6, 7])
        quantize_w(2)
        store([S, S])
        out_1_products(1, 7, [4, 5])
        collect_w(3, 0, [V, V])
        store([S, S])
        out_0_products(0, 0, [2, 3])
        collect_w(3, 1, [V, V])
        out_0_products(1, 0, [0, 1])
        store([S, S])
        out_0_products(2, 0, [4, 5])
        quantize_w(3)
        store([S, S])
        ring = [[6, 7], [2, 3], [0, 1], [4, 5]]
        for k in range(5):
            out_0_products((3 + k) % 4, min(k, 1), ring[k % 4])
            store([S, V])
        for k in range(2):
            store([S, V])
